import numpy as np
import ml_dtypes


def mxq(x, axis, fmt="e4m3"):
    dtype, down = {"e4m3": (ml_dtypes.float8_e4m3fn, 7), "e5m2": (ml_dtypes.float8_e5m2, 14)}[fmt]
    v = np.moveaxis(np.asarray(x, np.float32).astype(ml_dtypes.bfloat16).astype(np.float64), axis, -1)
    blocks = v.reshape(v.shape[:-1] + (-1, 32))
    amax = np.abs(blocks).max(-1, keepdims=True)
    byte = np.maximum(np.where(amax > 0, np.frexp(amax)[1] - 1 + 127, 0) - down, 1)
    scale = np.exp2(byte - 127.0)
    codes = (blocks / scale).astype(np.float32).astype(dtype).astype(np.float64)
    return np.moveaxis((codes * scale).reshape(v.shape), -1, axis)


WIDE = False


def mx_kscale(k):
    if not WIDE:
        return np.ones(k)
    levels = np.array([10, -10, 5, -5, 0])
    a = np.random.permutation(np.resize(levels, k // 512 * 4)).reshape(k // 512, 4)
    idx = np.arange(k)
    return np.exp2(a[idx // 512, idx % 128 // 32])


BF16 = ml_dtypes.bfloat16


def bf(x):
    return np.asarray(x, np.float32).astype(BF16)


def f64(x):
    return np.asarray(x).astype(np.float64)


SL, BS, DM, H, NH, DO = 32, 128, 1024, 16, 64, 1024
DP = H * NH


def setup_inputs():
    s, t = mx_kscale(DM), mx_kscale(DP)
    g = np.random.standard_normal((SL, BS, H)) * 2.0
    return {"values": bf(np.random.standard_normal((SL, BS, DM)) * s),
            "logw": bf(g - np.log(np.exp(g).sum(0, keepdims=True))),
            "Wv": bf(np.random.standard_normal((DP, DM)) / np.sqrt(DM * SL) / s * t[:, None]),
            "Wo": bf(np.random.standard_normal((DO, DP)) * 0.5 / np.sqrt(DP) / t)}


def reference(values, logw, Wv, Wo):
    vp = mxq(f64(values), 2, "e4m3") @ mxq(f64(Wv), 1, "e4m3").T
    attn = (f64(logw)[..., None] * vp.reshape(SL, BS, H, NH)).sum(0)
    return mxq(attn.reshape(BS, DP), 1, "e4m3") @ mxq(f64(Wo), 1, "e4m3").T

@@ -1,0 +1,232 @@
+from contextlib import ExitStack
+
+import concourse.mybir as mybir
+from concourse.masks import make_identity
+
+F32 = mybir.dt.float32
+BF16 = mybir.dt.bfloat16
+U32 = mybir.dt.uint32
+U8 = mybir.dt.uint8
+FP8X4 = mybir.dt.float8_e4m3fn_x4
+MULT = mybir.AluOpType.mult
+ADD = mybir.AluOpType.add
+
+P = 128
+SL, DM, HEADS, HEAD_DIM, DO = 32, 1024, 16, 64, 1024
+DP = HEADS * HEAD_DIM
+K_PASS = 512
+PASSES = DM // K_PASS
+N_TILE = 512
+HALVES = DP // N_TILE
+HEADS_PER_HALF = N_TILE // HEAD_DIM
+GROUP = 4
+N_GROUPS = SL // GROUP
+WORDS = DM // 2
+
+FLOPS = 2 * SL * P * DM * DP + 2 * P * DP * DO
+
+
+def tile_multiheadattention_pb_kernel(tc, values, logw, Wv, Wo, out):
+    nc = tc.nc
+    with ExitStack() as ctx:
+        keep = ctx.enter_context(tc.tile_pool(name="keep", bufs=1))
+        stage = ctx.enter_context(tc.tile_pool(name="stage", bufs=2))
+        sums_psum = ctx.enter_context(tc.psum_pool(name="sums", bufs=4))
+        ctx.enter_context(tc.manual_schedule())
+
+        ident = keep.tile([P, P], F32)
+        make_identity(nc, ident[:])
+        acc = keep.tile([P, DP], F32)
+        nc.vector.memset(acc[:], 0.0)
+
+        x_raw = [keep.tile([P, GROUP * DM], BF16, name="x_raw%d" % i) for i in range(N_GROUPS)]
+        w_raw = [keep.tile([P, GROUP * DM], BF16, name="w_raw%d" % i) for i in range(2 * HALVES)]
+        lw_bf = keep.tile([P, SL, HEADS], BF16)
+        lw = keep.tile([P, SL, HEADS], F32)
+        val_codes = keep.tile([P, SL * PASSES * P], U32, align_bytes=64)
+        val_scales = keep.tile([P, SL * PASSES * P], U8, align_bytes=64)
+        wv_codes = keep.tile([P, PASSES * DP], U32, align_bytes=64)
+        wv_scales = keep.tile([P, PASSES * DP], U8, align_bytes=64)
+        wo_codes = keep.tile([P, PASSES * DO], U32, align_bytes=64)
+        wo_scales = keep.tile([P, PASSES * DO], U8, align_bytes=64)
+        attn_grouped = keep.tile([P, PASSES * P * 4], BF16, align_bytes=64)
+        attn_codes = keep.tile([P, PASSES * P], U32, align_bytes=64)
+        attn_scales = keep.tile([P, PASSES * P], U8, align_bytes=64)
+        out_sb = keep.tile([P, DO], F32)
+
+        weight_halves = [
+            (Wv, wv_codes, wv_scales, 0),
+            (Wv, wv_codes, wv_scales, 1),
+            (Wo, wo_codes, wo_scales, 0),
+            (Wo, wo_codes, wo_scales, 1),
+        ]
+
+        def load_units(raw, matrix, first_unit):
+            rows = matrix[first_unit * P : (first_unit + GROUP) * P, :]
+            src = rows.rearrange("(t p) k -> p t k", p=P)
+            dst = raw[:].rearrange("p (t k) -> p t k", t=GROUP)
+            for t in range(0, GROUP, 2):
+                nc.sync.dma_start(out=dst[:, t : t + 2, :], in_=src[:, t : t + 2, :])
+
+        def load_weight_half(w):
+            matrix, half = weight_halves[w][0], weight_halves[w][3]
+            load_units(w_raw[w], matrix, half * GROUP)
+
+        value_rows = values.flatten_outer_dims()
+        load_weight_half(0)
+        for i in range(N_GROUPS):
+            positions = slice(GROUP * i, GROUP * (i + 1))
+            nc.sync.dma_start(
+                out=lw_bf[:, positions, :], in_=logw[positions].rearrange("s b h -> b s h")
+            )
+            load_units(x_raw[i], value_rows, GROUP * i)
+            if i % 2 == 0 and i > 0:
+                load_weight_half(i // 2)
+
+        def flip_unit(flip_psum, rows, grouped_words):
+            words = rows.bitcast(F32)
+            flipped = flip_psum.tile([P, PASSES, 2, P], F32, tag="flipped")
+            for g in range(PASSES):
+                for u in range(2):
+                    first = (2 * g + u) * P
+                    nc.tensor.transpose(flipped[:, g, u, :], words[:, first : first + P], ident[:])
+            nc.scalar.copy(out=grouped_words, in_=flipped[:].rearrange("p g u r -> p g r u"))
+
+        def quantise(grouped, codes, scales):
+            nc.vector.quantize_mx(out=codes.bitcast(FP8X4), scales=scales, in_=grouped)
+
+        def flip_values(flip_psum, i):
+            grouped = stage.tile([P, GROUP * PASSES * P * 4], BF16, tag="x_grouped", align_bytes=64)
+            words = grouped[:].bitcast(F32).rearrange(
+                "p (t g r u) -> p t g r u", t=GROUP, g=PASSES, u=2
+            )
+            for t in range(GROUP):
+                flip_unit(flip_psum, x_raw[i][:, t * DM : (t + 1) * DM], words[:, t])
+            positions = slice(GROUP * i, GROUP * (i + 1))
+            nc.vector.tensor_copy(out=lw[:, positions, :], in_=lw_bf[:, positions, :])
+            return grouped
+
+        def quantise_values(grouped, i, pair):
+            n = 2 * PASSES * P
+            first = (GROUP * i + 2 * pair) * PASSES * P
+            quantise(
+                grouped[:, pair * 4 * n : (pair + 1) * 4 * n],
+                val_codes[:, first : first + n],
+                val_scales[:, first : first + n],
+            )
+
+        def new_weight_grouped():
+            grouped = stage.tile([P, PASSES * N_TILE * 4], BF16, tag="w_grouped", align_bytes=64)
+            return grouped
+
+        def flip_weight_units(flip_psum, grouped, w, units):
+            words = grouped[:].bitcast(F32).rearrange("p (g r u) -> p g r u", g=PASSES, u=2)
+            for t in units:
+                flip_unit(
+                    flip_psum, w_raw[w][:, t * DM : (t + 1) * DM], words[:, :, t * P : (t + 1) * P, :]
+                )
+
+        def quantise_weight_half(grouped, w):
+            codes, scales, half = weight_halves[w][1], weight_halves[w][2], weight_halves[w][3]
+            for g in range(PASSES):
+                first = g * DP + half * N_TILE
+                quantise(
+                    grouped[:, g * 4 * N_TILE : (g + 1) * 4 * N_TILE],
+                    codes[:, first : first + N_TILE],
+                    scales[:, first : first + N_TILE],
+                )
+
+        def project_and_pool(s, half):
+            vp = sums_psum.tile([P, N_TILE], F32, tag="vp")
+            for g in range(PASSES):
+                rows = slice((s * PASSES + g) * P, (s * PASSES + g + 1) * P)
+                cols = slice(g * DP + half * N_TILE, g * DP + (half + 1) * N_TILE)
+                nc.tensor.matmul_mx(
+                    out=vp[:],
+                    lhsT=val_codes[:, rows].bitcast(FP8X4),
+                    lhsT_scale=val_scales[:, rows],
+                    rhs=wv_codes[:, cols].bitcast(FP8X4),
+                    rhs_scale=wv_scales[:, cols],
+                    start=(g == 0),
+                    stop=(g == PASSES - 1),
+                )
+            for j in range(HEADS_PER_HALF):
+                h = half * HEADS_PER_HALF + j
+                channels = slice(h * HEAD_DIM, (h + 1) * HEAD_DIM)
+                nc.vector.scalar_tensor_tensor(
+                    out=acc[:, channels],
+                    in0=vp[:, j * HEAD_DIM : (j + 1) * HEAD_DIM],
+                    scalar=lw[:, s, h : h + 1],
+                    in1=acc[:, channels],
+                    op0=MULT,
+                    op1=ADD,
+                )
+
+        with tc.psum_pool(name="flip", bufs=4) as flip_psum:
+            w_grouped = new_weight_grouped()
+            flip_weight_units(flip_psum, w_grouped, 0, range(GROUP))
+            quantise_weight_half(w_grouped, 0)
+            x_grouped = flip_values(flip_psum, 0)
+            quantise_values(x_grouped, 0, 0)
+            quantise_values(x_grouped, 0, 1)
+
+            for i in range(N_GROUPS):
+                if i + 1 < N_GROUPS:
+                    x_grouped = flip_values(flip_psum, i + 1)
+                if i >= 2:
+                    if i % 2 == 0:
+                        w_grouped = new_weight_grouped()
+                    first_unit = (i % 2) * 2
+                    flip_weight_units(flip_psum, w_grouped, i // 2, range(first_unit, first_unit + 2))
+                for t in range(GROUP):
+                    project_and_pool(GROUP * i + t, 0)
+                    if t % 2 == 1 and i + 1 < N_GROUPS:
+                        quantise_values(x_grouped, i + 1, t // 2)
+                if i >= 2 and i % 2 == 1:
+                    quantise_weight_half(w_grouped, i // 2)
+
+        with tc.psum_pool(name="second", bufs=1) as second_psum:
+            out_sums = [second_psum.tile([P, N_TILE], F32, name="out_sums%d" % n) for n in range(HALVES)]
+
+            def attn_to_mx(g):
+                flipped = second_psum.tile([P, 4, P], F32, name="attn_flipped%d" % g)
+                pairs = acc[:].rearrange("b (w e) -> b e w", e=2)
+                for t in range(4):
+                    first = (2 * g + t // 2) * P
+                    nc.tensor.transpose(flipped[:, t, :], pairs[:, t % 2, first : first + P], ident[:])
+                grouped = attn_grouped[:, g * 4 * P : (g + 1) * 4 * P]
+                nc.scalar.copy(
+                    out=grouped.rearrange("p (b t) -> p b t", t=4),
+                    in_=flipped[:].rearrange("p t b -> p b t"),
+                )
+                quantise(
+                    grouped, attn_codes[:, g * P : (g + 1) * P], attn_scales[:, g * P : (g + 1) * P]
+                )
+
+            def output_passes(g):
+                for n in range(HALVES):
+                    cols = slice(g * DO + n * N_TILE, g * DO + (n + 1) * N_TILE)
+                    nc.tensor.matmul_mx(
+                        out=out_sums[n][:],
+                        lhsT=attn_codes[:, g * P : (g + 1) * P].bitcast(FP8X4),
+                        lhsT_scale=attn_scales[:, g * P : (g + 1) * P],
+                        rhs=wo_codes[:, cols].bitcast(FP8X4),
+                        rhs_scale=wo_scales[:, cols],
+                        start=(g == 0),
+                        stop=(g == PASSES - 1),
+                    )
+
+            for i in range(N_GROUPS):
+                for t in range(GROUP):
+                    project_and_pool(GROUP * i + t, 1)
+                if i == 0:
+                    attn_to_mx(0)
+                if i == 1:
+                    output_passes(0)
+            attn_to_mx(1)
+            output_passes(1)
+
+            nc.scalar.copy(out=out_sb[:, 0:N_TILE], in_=out_sums[0][:])
+            nc.sync.dma_start(out=out[:, 0:N_TILE], in_=out_sb[:, 0:N_TILE])
+            nc.vector.tensor_copy(out=out_sb[:, N_TILE:DO], in_=out_sums[1][:])
+            nc.sync.dma_start(out=out[:, N_TILE:DO], in_=out_sb[:, N_TILE:DO])

@@ -10,6 +10,7 @@ U8 = mybir.dt.uint8
 FP8X4 = mybir.dt.float8_e4m3fn_x4
 MULT = mybir.AluOpType.mult
 ADD = mybir.AluOpType.add
+COPY = mybir.ActivationFunctionType.Copy
 
 P = 128
 SL, DM, HEADS, HEAD_DIM, DO = 32, 1024, 16, 64, 1024
@@ -38,6 +39,8 @@ def tile_multiheadattention_pb_kernel(tc, values, logw, Wv, Wo, out):
         make_identity(nc, ident[:])
         acc = keep.tile([P, DP], F32)
         nc.vector.memset(acc[:], 0.0)
+        acc_side = keep.tile([P, DP], F32)
+        nc.gpsimd.memset(acc_side[:], 0.0)
 
         x_raw = [keep.tile([P, GROUP * DM], BF16, name="x_raw%d" % i) for i in range(N_GROUPS)]
         w_raw = [keep.tile([P, GROUP * DM], BF16, name="w_raw%d" % i) for i in range(2 * HALVES)]
@@ -136,7 +139,7 @@ def tile_multiheadattention_pb_kernel(tc, values, logw, Wv, Wo, out):
                     scales[:, first : first + N_TILE],
                 )
 
-        def project_and_pool(s, half):
+        def project_and_pool(s, half, on_the_side):
             vp = sums_psum.tile([P, N_TILE], F32, tag="vp")
             for g in range(PASSES):
                 rows = slice((s * PASSES + g) * P, (s * PASSES + g + 1) * P)
@@ -150,17 +153,37 @@ def tile_multiheadattention_pb_kernel(tc, values, logw, Wv, Wo, out):
                     start=(g == 0),
                     stop=(g == PASSES - 1),
                 )
+            if on_the_side:
+                weighted = stage.tile([P, N_TILE], F32, tag="weighted")
             for j in range(HEADS_PER_HALF):
                 h = half * HEADS_PER_HALF + j
                 channels = slice(h * HEAD_DIM, (h + 1) * HEAD_DIM)
-                nc.vector.scalar_tensor_tensor(
-                    out=acc[:, channels],
-                    in0=vp[:, j * HEAD_DIM : (j + 1) * HEAD_DIM],
-                    scalar=lw[:, s, h : h + 1],
-                    in1=acc[:, channels],
-                    op0=MULT,
-                    op1=ADD,
-                )
+                bank_cols = slice(j * HEAD_DIM, (j + 1) * HEAD_DIM)
+                if on_the_side:
+                    nc.scalar.activation(
+                        out=weighted[:, bank_cols], in_=vp[:, bank_cols], func=COPY, scale=lw[:, s, h : h + 1]
+                    )
+                else:
+                    nc.vector.scalar_tensor_tensor(
+                        out=acc[:, channels],
+                        in0=vp[:, bank_cols],
+                        scalar=lw[:, s, h : h + 1],
+                        in1=acc[:, channels],
+                        op0=MULT,
+                        op1=ADD,
+                    )
+            if on_the_side:
+                side = acc_side[:, half * N_TILE : (half + 1) * N_TILE]
+                nc.gpsimd.tensor_tensor(out=side, in0=side, in1=weighted[:], op=ADD)
+
+        def project_group(i, half, after_position):
+            last = i == N_GROUPS - 1
+            if last:
+                cols = slice(half * N_TILE, (half + 1) * N_TILE)
+                nc.vector.tensor_tensor(out=acc[:, cols], in0=acc[:, cols], in1=acc_side[:, cols], op=ADD)
+            for t in range(GROUP):
+                project_and_pool(GROUP * i + t, half, t == 0 and not last)
+                after_position(t)
 
         with tc.psum_pool(name="flip", bufs=4) as flip_psum:
             w_grouped = new_weight_grouped()
@@ -178,10 +201,11 @@ def tile_multiheadattention_pb_kernel(tc, values, logw, Wv, Wo, out):
                         w_grouped = new_weight_grouped()
                     first_unit = (i % 2) * 2
                     flip_weight_units(flip_psum, w_grouped, i // 2, range(first_unit, first_unit + 2))
-                for t in range(GROUP):
-                    project_and_pool(GROUP * i + t, 0)
+                def quantise_next(t):
                     if t % 2 == 1 and i + 1 < N_GROUPS:
                         quantise_values(x_grouped, i + 1, t // 2)
+
+                project_group(i, 0, quantise_next)
                 if i >= 2 and i % 2 == 1:
                     quantise_weight_half(w_grouped, i // 2)
 
@@ -217,8 +241,7 @@ def tile_multiheadattention_pb_kernel(tc, values, logw, Wv, Wo, out):
                     )
 
             for i in range(N_GROUPS):
-                for t in range(GROUP):
-                    project_and_pool(GROUP * i + t, 1)
+                project_group(i, 1, lambda t: None)
                 if i == 0:
                     attn_to_mx(0)
                 if i == 1:

@@ -22,7 +22,8 @@ HALVES = DP // N_TILE
 HEADS_PER_HALF = N_TILE // HEAD_DIM
 GROUP = 4
 N_GROUPS = SL // GROUP
-WORDS = DM // 2
+W_UNITS = DP // P
+UNIT_WORDS = PASSES * P
 
 FLOPS = 2 * SL * P * DM * DP + 2 * P * DP * DO
 
@@ -43,48 +44,45 @@ def tile_multiheadattention_pb_kernel(tc, values, logw, Wv, Wo, out):
         nc.gpsimd.memset(acc_side[:], 0.0)
 
         x_raw = [keep.tile([P, GROUP * DM], BF16, name="x_raw%d" % i) for i in range(N_GROUPS)]
-        w_raw = [keep.tile([P, GROUP * DM], BF16, name="w_raw%d" % i) for i in range(2 * HALVES)]
+        wv_raw = keep.tile([P, W_UNITS * DM], BF16)
+        wo_raw = keep.tile([P, W_UNITS * DM], BF16)
         lw_bf = keep.tile([P, SL, HEADS], BF16)
         lw = keep.tile([P, SL, HEADS], F32)
-        val_codes = keep.tile([P, SL * PASSES * P], U32, align_bytes=64)
-        val_scales = keep.tile([P, SL * PASSES * P], U8, align_bytes=64)
+        val_codes = keep.tile([P, SL * UNIT_WORDS], U32, align_bytes=64)
+        val_scales = keep.tile([P, SL * UNIT_WORDS], U8, align_bytes=64)
         wv_codes = keep.tile([P, PASSES * DP], U32, align_bytes=64)
         wv_scales = keep.tile([P, PASSES * DP], U8, align_bytes=64)
         wo_codes = keep.tile([P, PASSES * DO], U32, align_bytes=64)
         wo_scales = keep.tile([P, PASSES * DO], U8, align_bytes=64)
-        attn_grouped = keep.tile([P, PASSES * P * 4], BF16, align_bytes=64)
-        attn_codes = keep.tile([P, PASSES * P], U32, align_bytes=64)
-        attn_scales = keep.tile([P, PASSES * P], U8, align_bytes=64)
+        attn_grouped = keep.tile([P, 4 * UNIT_WORDS], BF16, align_bytes=64)
+        attn_codes = keep.tile([P, UNIT_WORDS], U32, align_bytes=64)
+        attn_scales = keep.tile([P, UNIT_WORDS], U8, align_bytes=64)
         out_sb = keep.tile([P, DO], F32)
 
-        weight_halves = [
-            (Wv, wv_codes, wv_scales, 0),
-            (Wv, wv_codes, wv_scales, 1),
-            (Wo, wo_codes, wo_scales, 0),
-            (Wo, wo_codes, wo_scales, 1),
-        ]
-
-        def load_units(raw, matrix, first_unit):
-            rows = matrix[first_unit * P : (first_unit + GROUP) * P, :]
-            src = rows.rearrange("(t p) k -> p t k", p=P)
-            dst = raw[:].rearrange("p (t k) -> p t k", t=GROUP)
-            for t in range(0, GROUP, 2):
-                nc.sync.dma_start(out=dst[:, t : t + 2, :], in_=src[:, t : t + 2, :])
-
-        def load_weight_half(w):
-            matrix, half = weight_halves[w][0], weight_halves[w][3]
-            load_units(w_raw[w], matrix, half * GROUP)
+        def load_two_units(raw, slot, matrix, unit):
+            src = matrix[unit * P : (unit + 2) * P, :].rearrange("(t p) k -> p t k", p=P)
+            dst = raw[:, slot * DM : (slot + 2) * DM].rearrange("p (t k) -> p t k", t=2)
+            nc.sync.dma_start(out=dst, in_=src)
 
         value_rows = values.flatten_outer_dims()
-        load_weight_half(0)
-        for i in range(N_GROUPS):
+
+        def load_group(i):
             positions = slice(GROUP * i, GROUP * (i + 1))
             nc.sync.dma_start(
                 out=lw_bf[:, positions, :], in_=logw[positions].rearrange("s b h -> b s h")
             )
-            load_units(x_raw[i], value_rows, GROUP * i)
-            if i % 2 == 0 and i > 0:
-                load_weight_half(i // 2)
+            for t in range(0, GROUP, 2):
+                load_two_units(x_raw[i], t, value_rows, GROUP * i + t)
+
+        for u in range(0, W_UNITS // 2, 2):
+            load_two_units(wv_raw, u, Wv, u)
+        load_group(0)
+        for u in range(W_UNITS // 2, W_UNITS, 2):
+            load_two_units(wv_raw, u, Wv, u)
+        for i in range(1, N_GROUPS):
+            load_group(i)
+            if i % 2 == 1:
+                load_two_units(wo_raw, i - 1, Wo, i - 1)
 
         def flip_unit(flip_psum, rows, grouped_words):
             words = rows.bitcast(F32)
@@ -99,7 +97,7 @@ def tile_multiheadattention_pb_kernel(tc, values, logw, Wv, Wo, out):
             nc.vector.quantize_mx(out=codes.bitcast(FP8X4), scales=scales, in_=grouped)
 
         def flip_values(flip_psum, i):
-            grouped = stage.tile([P, GROUP * PASSES * P * 4], BF16, tag="x_grouped", align_bytes=64)
+            grouped = stage.tile([P, GROUP * 4 * UNIT_WORDS], BF16, tag="x_grouped", align_bytes=64)
             words = grouped[:].bitcast(F32).rearrange(
                 "p (t g r u) -> p t g r u", t=GROUP, g=PASSES, u=2
             )
@@ -110,33 +108,27 @@ def tile_multiheadattention_pb_kernel(tc, values, logw, Wv, Wo, out):
             return grouped
 
         def quantise_values(grouped, i, pair):
-            n = 2 * PASSES * P
-            first = (GROUP * i + 2 * pair) * PASSES * P
+            n = 2 * UNIT_WORDS
+            first = (GROUP * i + 2 * pair) * UNIT_WORDS
             quantise(
                 grouped[:, pair * 4 * n : (pair + 1) * 4 * n],
                 val_codes[:, first : first + n],
                 val_scales[:, first : first + n],
             )
 
-        def new_weight_grouped():
-            grouped = stage.tile([P, PASSES * N_TILE * 4], BF16, tag="w_grouped", align_bytes=64)
+        def flip_weight_unit(flip_psum, raw, unit):
+            grouped = stage.tile([P, 4 * UNIT_WORDS], BF16, tag="w_grouped", bufs=3, align_bytes=64)
+            words = grouped[:].bitcast(F32).rearrange("p (g r u) -> p g r u", g=PASSES, u=2)
+            flip_unit(flip_psum, raw[:, unit * DM : (unit + 1) * DM], words)
             return grouped
 
-        def flip_weight_units(flip_psum, grouped, w, units):
-            words = grouped[:].bitcast(F32).rearrange("p (g r u) -> p g r u", g=PASSES, u=2)
-            for t in units:
-                flip_unit(
-                    flip_psum, w_raw[w][:, t * DM : (t + 1) * DM], words[:, :, t * P : (t + 1) * P, :]
-                )
-
-        def quantise_weight_half(grouped, w):
-            codes, scales, half = weight_halves[w][1], weight_halves[w][2], weight_halves[w][3]
+        def quantise_weight_unit(grouped, codes, scales, unit):
             for g in range(PASSES):
-                first = g * DP + half * N_TILE
+                first = g * DP + unit * P
                 quantise(
-                    grouped[:, g * 4 * N_TILE : (g + 1) * 4 * N_TILE],
-                    codes[:, first : first + N_TILE],
-                    scales[:, first : first + N_TILE],
+                    grouped[:, g * 4 * P : (g + 1) * 4 * P],
+                    codes[:, first : first + P],
+                    scales[:, first : first + P],
                 )
 
         def project_and_pool(s, half, on_the_side):
@@ -176,45 +168,43 @@ def tile_multiheadattention_pb_kernel(tc, values, logw, Wv, Wo, out):
                 side = acc_side[:, half * N_TILE : (half + 1) * N_TILE]
                 nc.gpsimd.tensor_tensor(out=side, in0=side, in1=weighted[:], op=ADD)
 
-        def project_group(i, half, after_position):
-            last = i == N_GROUPS - 1
-            if last:
-                cols = slice(half * N_TILE, (half + 1) * N_TILE)
-                nc.vector.tensor_tensor(out=acc[:, cols], in0=acc[:, cols], in1=acc_side[:, cols], op=ADD)
-            for t in range(GROUP):
-                project_and_pool(GROUP * i + t, half, t == 0 and not last)
-                after_position(t)
+        def join_sums(half):
+            cols = slice(half * N_TILE, (half + 1) * N_TILE)
+            nc.gpsimd.tensor_tensor(out=acc[:, cols], in0=acc[:, cols], in1=acc_side[:, cols], op=ADD)
 
         with tc.psum_pool(name="flip", bufs=4) as flip_psum:
-            w_grouped = new_weight_grouped()
-            flip_weight_units(flip_psum, w_grouped, 0, range(GROUP))
-            quantise_weight_half(w_grouped, 0)
+            for unit in range(W_UNITS // 2):
+                w_grouped = flip_weight_unit(flip_psum, wv_raw, unit)
+                quantise_weight_unit(w_grouped, wv_codes, wv_scales, unit)
             x_grouped = flip_values(flip_psum, 0)
             quantise_values(x_grouped, 0, 0)
             quantise_values(x_grouped, 0, 1)
+            for unit in range(W_UNITS // 2, W_UNITS):
+                w_grouped = flip_weight_unit(flip_psum, wv_raw, unit)
+                quantise_weight_unit(w_grouped, wv_codes, wv_scales, unit)
 
             for i in range(N_GROUPS):
-                if i + 1 < N_GROUPS:
+                more_values = i + 1 < N_GROUPS
+                if not more_values:
+                    join_sums(1)
+                for t in range(GROUP):
+                    project_and_pool(GROUP * i + t, 0, t == 0)
+                if not more_values:
+                    join_sums(0)
+                if more_values:
                     x_grouped = flip_values(flip_psum, i + 1)
-                if i >= 2:
-                    if i % 2 == 0:
-                        w_grouped = new_weight_grouped()
-                    first_unit = (i % 2) * 2
-                    flip_weight_units(flip_psum, w_grouped, i // 2, range(first_unit, first_unit + 2))
-                def quantise_next(t):
-                    if t % 2 == 1 and i + 1 < N_GROUPS:
-                        quantise_values(x_grouped, i + 1, t // 2)
-
-                project_group(i, 0, quantise_next)
-                if i >= 2 and i % 2 == 1:
-                    quantise_weight_half(w_grouped, i // 2)
+                w_grouped = flip_weight_unit(flip_psum, wo_raw, i)
+                for t in range(GROUP):
+                    if t < 2 and more_values:
+                        quantise_values(x_grouped, i + 1, t)
+                    if t == 2:
+                        quantise_weight_unit(w_grouped, wo_codes, wo_scales, i)
+                    project_and_pool(GROUP * i + t, 1, t == 1 and more_values)
 
         with tc.psum_pool(name="second", bufs=1) as second_psum:
-            out_sums = [second_psum.tile([P, N_TILE], F32, name="out_sums%d" % n) for n in range(HALVES)]
-
-            def attn_to_mx(g):
+            pairs = acc[:].rearrange("b (w e) -> b e w", e=2)
+            for g in range(PASSES):
                 flipped = second_psum.tile([P, 4, P], F32, name="attn_flipped%d" % g)
-                pairs = acc[:].rearrange("b (w e) -> b e w", e=2)
                 for t in range(4):
                     first = (2 * g + t // 2) * P
                     nc.tensor.transpose(flipped[:, t, :], pairs[:, t % 2, first : first + P], ident[:])
@@ -226,8 +216,8 @@ def tile_multiheadattention_pb_kernel(tc, values, logw, Wv, Wo, out):
                 quantise(
                     grouped, attn_codes[:, g * P : (g + 1) * P], attn_scales[:, g * P : (g + 1) * P]
                 )
-
-            def output_passes(g):
+            out_sums = [second_psum.tile([P, N_TILE], F32, name="out_sums%d" % n) for n in range(HALVES)]
+            for g in range(PASSES):
                 for n in range(HALVES):
                     cols = slice(g * DO + n * N_TILE, g * DO + (n + 1) * N_TILE)
                     nc.tensor.matmul_mx(
@@ -239,16 +229,6 @@ def tile_multiheadattention_pb_kernel(tc, values, logw, Wv, Wo, out):
                         start=(g == 0),
                         stop=(g == PASSES - 1),
                     )
-
-            for i in range(N_GROUPS):
-                project_group(i, 1, lambda t: None)
-                if i == 0:
-                    attn_to_mx(0)
-                if i == 1:
-                    output_passes(0)
-            attn_to_mx(1)
-            output_passes(1)
-
             nc.scalar.copy(out=out_sb[:, 0:N_TILE], in_=out_sums[0][:])
             nc.sync.dma_start(out=out[:, 0:N_TILE], in_=out_sb[:, 0:N_TILE])
             nc.vector.tensor_copy(out=out_sb[:, N_TILE:DO], in_=out_sums[1][:])

@@ -10,7 +10,6 @@ U8 = mybir.dt.uint8
 FP8X4 = mybir.dt.float8_e4m3fn_x4
 MULT = mybir.AluOpType.mult
 ADD = mybir.AluOpType.add
-COPY = mybir.ActivationFunctionType.Copy
 
 P = 128
 SL, DM, HEADS, HEAD_DIM, DO = 32, 1024, 16, 64, 1024
@@ -40,8 +39,6 @@ def tile_multiheadattention_pb_kernel(tc, values, logw, Wv, Wo, out):
         make_identity(nc, ident[:])
         acc = keep.tile([P, DP], F32)
         nc.vector.memset(acc[:], 0.0)
-        acc_side = keep.tile([P, DP], F32)
-        nc.gpsimd.memset(acc_side[:], 0.0)
 
         x_raw = [keep.tile([P, GROUP * DM], BF16, name="x_raw%d" % i) for i in range(N_GROUPS)]
         wv_raw = keep.tile([P, W_UNITS * DM], BF16)
@@ -131,7 +128,7 @@ def tile_multiheadattention_pb_kernel(tc, values, logw, Wv, Wo, out):
                     scales[:, first : first + P],
                 )
 
-        def project_and_pool(s, half, on_the_side):
+        def project_and_pool(s, half):
             vp = sums_psum.tile([P, N_TILE], F32, tag="vp")
             for g in range(PASSES):
                 rows = slice((s * PASSES + g) * P, (s * PASSES + g + 1) * P)
@@ -145,32 +142,18 @@ def tile_multiheadattention_pb_kernel(tc, values, logw, Wv, Wo, out):
                     start=(g == 0),
                     stop=(g == PASSES - 1),
                 )
-            if on_the_side:
-                weighted = stage.tile([P, N_TILE], F32, tag="weighted")
             for j in range(HEADS_PER_HALF):
                 h = half * HEADS_PER_HALF + j
                 channels = slice(h * HEAD_DIM, (h + 1) * HEAD_DIM)
                 bank_cols = slice(j * HEAD_DIM, (j + 1) * HEAD_DIM)
-                if on_the_side:
-                    nc.scalar.activation(
-                        out=weighted[:, bank_cols], in_=vp[:, bank_cols], func=COPY, scale=lw[:, s, h : h + 1]
-                    )
-                else:
-                    nc.vector.scalar_tensor_tensor(
-                        out=acc[:, channels],
-                        in0=vp[:, bank_cols],
-                        scalar=lw[:, s, h : h + 1],
-                        in1=acc[:, channels],
-                        op0=MULT,
-                        op1=ADD,
-                    )
-            if on_the_side:
-                side = acc_side[:, half * N_TILE : (half + 1) * N_TILE]
-                nc.gpsimd.tensor_tensor(out=side, in0=side, in1=weighted[:], op=ADD)
-
-        def join_sums(half):
-            cols = slice(half * N_TILE, (half + 1) * N_TILE)
-            nc.gpsimd.tensor_tensor(out=acc[:, cols], in0=acc[:, cols], in1=acc_side[:, cols], op=ADD)
+                nc.vector.scalar_tensor_tensor(
+                    out=acc[:, channels],
+                    in0=vp[:, bank_cols],
+                    scalar=lw[:, s, h : h + 1],
+                    in1=acc[:, channels],
+                    op0=MULT,
+                    op1=ADD,
+                )
 
         with tc.psum_pool(name="flip", bufs=4) as flip_psum:
             for unit in range(W_UNITS // 2):
@@ -185,12 +168,8 @@ def tile_multiheadattention_pb_kernel(tc, values, logw, Wv, Wo, out):
 
             for i in range(N_GROUPS):
                 more_values = i + 1 < N_GROUPS
-                if not more_values:
-                    join_sums(1)
                 for t in range(GROUP):
-                    project_and_pool(GROUP * i + t, 0, t == 0)
-                if not more_values:
-                    join_sums(0)
+                    project_and_pool(GROUP * i + t, 0)
                 if more_values:
                     x_grouped = flip_values(flip_psum, i + 1)
                 w_grouped = flip_weight_unit(flip_psum, wo_raw, i)
@@ -199,7 +178,7 @@ def tile_multiheadattention_pb_kernel(tc, values, logw, Wv, Wo, out):
                         quantise_values(x_grouped, i + 1, t)
                     if t == 2:
                         quantise_weight_unit(w_grouped, wo_codes, wo_scales, i)
-                    project_and_pool(GROUP * i + t, 1, t == 1 and more_values)
+                    project_and_pool(GROUP * i + t, 1)
 
         with tc.psum_pool(name="second", bufs=1) as second_psum:
             pairs = acc[:].rearrange("b (w e) -> b e w", e=2)

from contextlib import ExitStack

import concourse.mybir as mybir
from concourse.masks import make_identity

F32 = mybir.dt.float32
BF16 = mybir.dt.bfloat16
U32 = mybir.dt.uint32
U8 = mybir.dt.uint8
FP8X4 = mybir.dt.float8_e4m3fn_x4
MULT = mybir.AluOpType.mult
ADD = mybir.AluOpType.add

P = 128
SL, DM, HEADS, HEAD_DIM, DO = 32, 1024, 16, 64, 1024
DP = HEADS * HEAD_DIM
K_PASS = 512
PASSES = DM // K_PASS
N_TILE = 512
HALVES = DP // N_TILE
HEADS_PER_HALF = N_TILE // HEAD_DIM
GROUP = 4
N_GROUPS = SL // GROUP
W_UNITS = DP // P
UNIT_WORDS = PASSES * P

FLOPS = 2 * SL * P * DM * DP + 2 * P * DP * DO


def tile_multiheadattention_pb_kernel(tc, values, logw, Wv, Wo, out):
    nc = tc.nc
    with ExitStack() as ctx:
        keep = ctx.enter_context(tc.tile_pool(name="keep", bufs=1))
        stage = ctx.enter_context(tc.tile_pool(name="stage", bufs=2))
        sums_psum = ctx.enter_context(tc.psum_pool(name="sums", bufs=4))
        ctx.enter_context(tc.manual_schedule())

        ident = keep.tile([P, P], F32)
        make_identity(nc, ident[:])
        acc = keep.tile([P, DP], F32)
        nc.vector.memset(acc[:], 0.0)

        x_raw = [keep.tile([P, GROUP * DM], BF16, name="x_raw%d" % i) for i in range(N_GROUPS)]
        wv_raw = keep.tile([P, W_UNITS * DM], BF16)
        wo_raw = keep.tile([P, W_UNITS * DM], BF16)
        lw_bf = keep.tile([P, SL, HEADS], BF16)
        lw = keep.tile([P, SL, HEADS], F32)
        val_codes = keep.tile([P, SL * UNIT_WORDS], U32, align_bytes=64)
        val_scales = keep.tile([P, SL * UNIT_WORDS], U8, align_bytes=64)
        wv_codes = keep.tile([P, PASSES * DP], U32, align_bytes=64)
        wv_scales = keep.tile([P, PASSES * DP], U8, align_bytes=64)
        wo_codes = keep.tile([P, PASSES * DO], U32, align_bytes=64)
        wo_scales = keep.tile([P, PASSES * DO], U8, align_bytes=64)
        attn_grouped = keep.tile([P, 4 * UNIT_WORDS], BF16, align_bytes=64)
        attn_codes = keep.tile([P, UNIT_WORDS], U32, align_bytes=64)
        attn_scales = keep.tile([P, UNIT_WORDS], U8, align_bytes=64)
        out_sb = keep.tile([P, DO], F32)

        def load_two_units(raw, slot, matrix, unit):
            src = matrix[unit * P : (unit + 2) * P, :].rearrange("(t p) k -> p t k", p=P)
            dst = raw[:, slot * DM : (slot + 2) * DM].rearrange("p (t k) -> p t k", t=2)
            nc.sync.dma_start(out=dst, in_=src)

        value_rows = values.flatten_outer_dims()

        def load_group(i):
            positions = slice(GROUP * i, GROUP * (i + 1))
            nc.sync.dma_start(
                out=lw_bf[:, positions, :], in_=logw[positions].rearrange("s b h -> b s h")
            )
            for t in range(0, GROUP, 2):
                load_two_units(x_raw[i], t, value_rows, GROUP * i + t)

        for u in range(0, W_UNITS // 2, 2):
            load_two_units(wv_raw, u, Wv, u)
        load_group(0)
        for u in range(W_UNITS // 2, W_UNITS, 2):
            load_two_units(wv_raw, u, Wv, u)
        for i in range(1, N_GROUPS):
            load_group(i)
            if i % 2 == 1:
                load_two_units(wo_raw, i - 1, Wo, i - 1)

        def flip_unit(flip_psum, rows, grouped_words):
            words = rows.bitcast(F32)
            flipped = flip_psum.tile([P, PASSES, 2, P], F32, tag="flipped")
            for g in range(PASSES):
                for u in range(2):
                    first = (2 * g + u) * P
                    nc.tensor.transpose(flipped[:, g, u, :], words[:, first : first + P], ident[:])
            nc.scalar.copy(out=grouped_words, in_=flipped[:].rearrange("p g u r -> p g r u"))

        def quantise(grouped, codes, scales):
            nc.vector.quantize_mx(out=codes.bitcast(FP8X4), scales=scales, in_=grouped)

        def flip_values(flip_psum, i):
            grouped = stage.tile([P, GROUP * 4 * UNIT_WORDS], BF16, tag="x_grouped", align_bytes=64)
            words = grouped[:].bitcast(F32).rearrange(
                "p (t g r u) -> p t g r u", t=GROUP, g=PASSES, u=2
            )
            for t in range(GROUP):
                flip_unit(flip_psum, x_raw[i][:, t * DM : (t + 1) * DM], words[:, t])
            positions = slice(GROUP * i, GROUP * (i + 1))
            nc.vector.tensor_copy(out=lw[:, positions, :], in_=lw_bf[:, positions, :])
            return grouped

        def quantise_values(grouped, i, pair):
            n = 2 * UNIT_WORDS
            first = (GROUP * i + 2 * pair) * UNIT_WORDS
            quantise(
                grouped[:, pair * 4 * n : (pair + 1) * 4 * n],
                val_codes[:, first : first + n],
                val_scales[:, first : first + n],
            )

        def flip_weight_unit(flip_psum, raw, unit):
            grouped = stage.tile([P, 4 * UNIT_WORDS], BF16, tag="w_grouped", bufs=3, align_bytes=64)
            words = grouped[:].bitcast(F32).rearrange("p (g r u) -> p g r u", g=PASSES, u=2)
            flip_unit(flip_psum, raw[:, unit * DM : (unit + 1) * DM], words)
            return grouped

        def quantise_weight_unit(grouped, codes, scales, unit):
            for g in range(PASSES):
                first = g * DP + unit * P
                quantise(
                    grouped[:, g * 4 * P : (g + 1) * 4 * P],
                    codes[:, first : first + P],
                    scales[:, first : first + P],
                )

        def project_and_pool(s, half):
            vp = sums_psum.tile([P, N_TILE], F32, tag="vp")
            for g in range(PASSES):
                rows = slice((s * PASSES + g) * P, (s * PASSES + g + 1) * P)
                cols = slice(g * DP + half * N_TILE, g * DP + (half + 1) * N_TILE)
                nc.tensor.matmul_mx(
                    out=vp[:],
                    lhsT=val_codes[:, rows].bitcast(FP8X4),
                    lhsT_scale=val_scales[:, rows],
                    rhs=wv_codes[:, cols].bitcast(FP8X4),
                    rhs_scale=wv_scales[:, cols],
                    start=(g == 0),
                    stop=(g == PASSES - 1),
                )
            for j in range(HEADS_PER_HALF):
                h = half * HEADS_PER_HALF + j
                channels = slice(h * HEAD_DIM, (h + 1) * HEAD_DIM)
                bank_cols = slice(j * HEAD_DIM, (j + 1) * HEAD_DIM)
                nc.vector.scalar_tensor_tensor(
                    out=acc[:, channels],
                    in0=vp[:, bank_cols],
                    scalar=lw[:, s, h : h + 1],
                    in1=acc[:, channels],
                    op0=MULT,
                    op1=ADD,
                )

        with tc.psum_pool(name="flip", bufs=4) as flip_psum:
            for unit in range(W_UNITS // 2):
                w_grouped = flip_weight_unit(flip_psum, wv_raw, unit)
                quantise_weight_unit(w_grouped, wv_codes, wv_scales, unit)
            x_grouped = flip_values(flip_psum, 0)
            quantise_values(x_grouped, 0, 0)
            quantise_values(x_grouped, 0, 1)
            for unit in range(W_UNITS // 2, W_UNITS):
                w_grouped = flip_weight_unit(flip_psum, wv_raw, unit)
                quantise_weight_unit(w_grouped, wv_codes, wv_scales, unit)

            for i in range(N_GROUPS):
                more_values = i + 1 < N_GROUPS
                for t in range(GROUP):
                    project_and_pool(GROUP * i + t, 0)
                if more_values:
                    x_grouped = flip_values(flip_psum, i + 1)
                w_grouped = flip_weight_unit(flip_psum, wo_raw, i)
                for t in range(GROUP):
                    if t < 2 and more_values:
                        quantise_values(x_grouped, i + 1, t)
                    if t == 2:
                        quantise_weight_unit(w_grouped, wo_codes, wo_scales, i)
                    project_and_pool(GROUP * i + t, 1)

        with tc.psum_pool(name="second", bufs=1) as second_psum:
            pairs = acc[:].rearrange("b (w e) -> b e w", e=2)
            for g in range(PASSES):
                flipped = second_psum.tile([P, 4, P], F32, name="attn_flipped%d" % g)
                for t in range(4):
                    first = (2 * g + t // 2) * P
                    nc.tensor.transpose(flipped[:, t, :], pairs[:, t % 2, first : first + P], ident[:])
                grouped = attn_grouped[:, g * 4 * P : (g + 1) * 4 * P]
                nc.scalar.copy(
                    out=grouped.rearrange("p (b t) -> p b t", t=4),
                    in_=flipped[:].rearrange("p t b -> p b t"),
                )
                quantise(
                    grouped, attn_codes[:, g * P : (g + 1) * P], attn_scales[:, g * P : (g + 1) * P]
                )
            out_sums = [second_psum.tile([P, N_TILE], F32, name="out_sums%d" % n) for n in range(HALVES)]
            for g in range(PASSES):
                for n in range(HALVES):
                    cols = slice(g * DO + n * N_TILE, g * DO + (n + 1) * N_TILE)
                    nc.tensor.matmul_mx(
                        out=out_sums[n][:],
                        lhsT=attn_codes[:, g * P : (g + 1) * P].bitcast(FP8X4),
                        lhsT_scale=attn_scales[:, g * P : (g + 1) * P],
                        rhs=wo_codes[:, cols].bitcast(FP8X4),
                        rhs_scale=wo_scales[:, cols],
                        start=(g == 0),
                        stop=(g == PASSES - 1),
                    )
            nc.scalar.copy(out=out_sb[:, 0:N_TILE], in_=out_sums[0][:])
            nc.sync.dma_start(out=out[:, 0:N_TILE], in_=out_sb[:, 0:N_TILE])
            nc.vector.tensor_copy(out=out_sb[:, N_TILE:DO], in_=out_sums[1][:])
            nc.sync.dma_start(out=out[:, N_TILE:DO], in_=out_sb[:, N_TILE:DO])
